import numpy as np
import ml_dtypes


def mxq(x, axis, fmt="e4m3"):
    dtype, down = {"e4m3": (ml_dtypes.float8_e4m3fn, 7), "e5m2": (ml_dtypes.float8_e5m2, 14)}[fmt]
    v = np.moveaxis(np.asarray(x, np.float32).astype(ml_dtypes.bfloat16).astype(np.float64), axis, -1)
    blocks = v.reshape(v.shape[:-1] + (-1, 32))
    amax = np.abs(blocks).max(-1, keepdims=True)
    byte = np.maximum(np.where(amax > 0, np.frexp(amax)[1] - 1 + 127, 0) - down, 1)
    scale = np.exp2(byte - 127.0)
    codes = (blocks / scale).astype(np.float32).astype(dtype).astype(np.float64)
    return np.moveaxis((codes * scale).reshape(v.shape), -1, axis)


WIDE = False


def mx_kscale(k):
    if not WIDE:
        return np.ones(k)
    levels = np.array([10, -10, 5, -5, 0])
    a = np.random.permutation(np.resize(levels, k // 512 * 4)).reshape(k // 512, 4)
    idx = np.arange(k)
    return np.exp2(a[idx // 512, idx % 128 // 32])


BF16 = ml_dtypes.bfloat16


def bf(x):
    return np.asarray(x, np.float32).astype(BF16)


def f64(x):
    return np.asarray(x).astype(np.float64)


B, T, D, H, NUM_LAYERS = 4, 2048, 512, 512, 3
EPS = 1e-8


def setup_inputs():
    s = mx_kscale(D)
    return {"inv": bf(np.random.standard_normal((B, T, D)) * 0.5 * s),
            "Wk": bf(np.random.standard_normal((D, D)) * 2.0 / np.sqrt(D) / s[None, :]),
            "bk": bf(2.5 / np.sqrt(D) + 0.7 * np.random.standard_normal(D))}


def reference(inv, Wk, bk):
    flat = f64(inv).reshape(-1, D)
    out = (mxq(flat, 1, "e4m3") @ mxq(f64(Wk), 1, "e4m3").T) + f64(bk)
    sqrtD = np.sqrt(D)
    S = out.sum(-1, keepdims=True)
    norms = np.sqrt((out * out).sum(-1, keepdims=True))
    c = out * S / (np.maximum(np.abs(out) * sqrtD, EPS) * np.maximum(norms, EPS))
    diff = np.abs(c[1:] - c[:-1]).sum(0)
    return np.broadcast_to(diff, (D, D)).copy()

@@ -1,0 +1,314 @@
+import math
+from contextlib import ExitStack
+
+import concourse.mybir as mybir
+from concourse.masks import make_identity
+
+FLOPS = 2 * 8192 * 512 * 512
+
+F32 = mybir.dt.float32
+BF16 = mybir.dt.bfloat16
+U32 = mybir.dt.uint32
+U8 = mybir.dt.uint8
+FP8X4 = mybir.dt.float8_e4m3fn_x4
+ALU = mybir.AluOpType
+ACT = mybir.ActivationFunctionType
+AX = mybir.AxisListType
+
+P = 128
+D = 512
+NT = 64
+NG = 16
+EPS = 1e-8
+DELTA = EPS / math.sqrt(D)
+XI = 8
+
+
+def tile_dispatcher_pa_kernel(tc, inv, Wk, bk, out):
+    nc = tc.nc
+    rows = inv.flatten_outer_dims().rearrange("(p t) k -> p t k", t=NT)
+    with ExitStack() as ctx:
+        const = ctx.enter_context(tc.tile_pool(name="const", bufs=1))
+        work = ctx.enter_context(tc.tile_pool(name="work", bufs=2))
+        small = ctx.enter_context(tc.tile_pool(name="small", bufs=4))
+        psum = ctx.enter_context(tc.psum_pool(name="psum", bufs=2))
+
+        one = const.tile([P, 1], F32, name="one")
+        nc.vector.memset(one[:], 1.0)
+        warm = const.tile([P, 1], F32, name="warm")
+        nc.scalar.activation(out=warm[:], in_=one[:], func=ACT.Sqrt)
+        ident = const.tile([P, P], F32, name="ident")
+        make_identity(nc, ident[:])
+
+        w_sb = const.tile([P, 4, D], BF16, name="w_sb")
+        nc.sync.dma_start(out=w_sb[:], in_=Wk.rearrange("(a p) k -> p a k", p=P))
+        b_bf = const.tile([P, D], BF16, name="b_bf")
+        nc.scalar.dma_start(out=b_bf[:], in_=bk.partition_broadcast(P))
+        xs = []
+        for g in range(NG):
+            xg = const.tile([P, 4, D], BF16, name="x%d" % g)
+            nc.sync.dma_start(out=xg[:], in_=rows[:, 4 * g : 4 * g + 4, :])
+            xs.append(xg)
+        x64 = const.tile([P, D], BF16, name="x64")
+        nc.sync.dma_start(out=x64[0 : P - 1, :], in_=rows[1:P, 0, :])
+        nc.sync.dma_start(out=x64[P - 1 : P, :], in_=rows[P - 1 : P, NT - 1, :])
+        bias = const.tile([P, D], F32, name="bias")
+        nc.vector.tensor_copy(out=bias[:], in_=b_bf[:])
+        part = const.tile([P, 4, NG], F32, name="part")
+
+        srcs = {"w": [w_sb[:, a, :] for a in range(4)], "x": [x64[:, :]]}
+        for g in range(NG):
+            srcs[g] = [xs[g][:, a, :] for a in range(4)]
+        st = {}
+
+        def transposes(un):
+            n = len(srcs[un])
+            banks = []
+            for h0 in range(0, n, 2):
+                xt = psum.tile([P, 2, 2, P], F32, tag="xt", name="xt")
+                for h in range(min(2, n - h0)):
+                    words = srcs[un][h0 + h].bitcast(F32)
+                    for u in range(2):
+                        nc.tensor.transpose(xt[:, h, u, :], words[:, u * P : (u + 1) * P], ident[:])
+                banks.append(xt)
+            st[("xt", un)] = banks
+
+        def copy_out(un):
+            n = len(srcs[un])
+            grp = work.tile([P, 4 * D], BF16, tag="grp", name="grp", align_bytes=64)
+            gv = grp[:].bitcast(F32).rearrange("p (a r u) -> p a r u", a=4, r=P, u=2)
+            for b, xt in enumerate(st[("xt", un)]):
+                m = min(2, n - 2 * b)
+                nc.scalar.copy(
+                    out=gv[:, 2 * b : 2 * b + m, :, :],
+                    in_=xt[:, 0:m, :, :].rearrange("p h u r -> p h r u"),
+                )
+            st[("grp", un)] = grp
+
+        def quant(un):
+            n = len(srcs[un])
+            if un == "w":
+                codes = const.tile([P, D], U32, name="w_codes", align_bytes=64)
+                scl = const.tile([P, D], U8, name="w_scl", align_bytes=64)
+            else:
+                codes = work.tile([P, D], U32, tag="codes", name="codes", align_bytes=64)
+                scl = work.tile([P, D], U8, tag="scl", name="scl", align_bytes=64)
+            nc.vector.quantize_mx(
+                out=codes[:, 0 : n * P].bitcast(FP8X4),
+                scales=scl[:, 0 : n * P],
+                in_=st[("grp", un)][:, 0 : n * D],
+            )
+            st[("codes", un)] = codes
+            st[("scl", un)] = scl
+
+        def mx(un, a):
+            acc = psum.tile([P, D], F32, tag="acc", name="acc")
+            nc.tensor.matmul_mx(
+                out=acc[:],
+                lhsT=st[("codes", un)][:, a * P : (a + 1) * P].bitcast(FP8X4),
+                lhsT_scale=st[("scl", un)][:, a * P : (a + 1) * P],
+                rhs=st[("codes", "w")][:].bitcast(FP8X4),
+                rhs_scale=st[("scl", "w")][:],
+                start=True,
+                stop=True,
+            )
+            st[("acc", un, a)] = acc
+
+        def p1(un, a):
+            if a == 0:
+                st[("o", un)] = work.tile([P, 4, D], F32, tag="o", name="o")
+                st[("ssum", un)] = small.tile([P, 4], F32, tag="ssum", name="ssum")
+                st[("n2", un)] = small.tile([P, 4], F32, tag="n2", name="n2")
+            nc.vector.scalar_tensor_tensor(
+                out=st[("o", un)][:, a, :],
+                in0=st[("acc", un, a)][:],
+                scalar=1.0,
+                in1=bias[:],
+                op0=ALU.mult,
+                op1=ALU.add,
+                accum_out=st[("ssum", un)][:, a : a + 1],
+            )
+
+        def p2(un, a):
+            junk = work.tile([P, D], F32, tag="junk", name="junk")
+            nc.scalar.activation(
+                out=junk[:],
+                in_=st[("o", un)][:, a, :],
+                func=ACT.Square,
+                accum_out=st[("n2", un)][:, a : a + 1],
+            )
+
+        def tau(un):
+            n = len(srcs[un])
+            tt = work.tile([P, 4, D], F32, tag="tau", name="tt")
+            nc.vector.tensor_scalar(
+                out=tt[:, 0:n, :],
+                in0=st[("o", un)][:, 0:n, :],
+                scalar1=DELTA,
+                scalar2=-DELTA,
+                op0=ALU.min,
+                op1=ALU.max,
+            )
+            st[("tau", un)] = tt
+
+        def m2(un):
+            n = len(srcs[un])
+            mm = small.tile([P, 4], F32, tag="m2", name="mm")
+            nc.vector.tensor_scalar(
+                out=mm[:, 0:n], in0=st[("n2", un)][:, 0:n], scalar1=EPS * EPS, scalar2=None, op0=ALU.max
+            )
+            st[("m2", un)] = mm
+
+        def root(un):
+            n = len(srcs[un])
+            nn = small.tile([P, 4], F32, tag="nn", name="nn")
+            nc.scalar.activation(out=nn[:, 0:n], in_=st[("m2", un)][:, 0:n], func=ACT.Sqrt)
+            st[("nn", un)] = nn
+
+        def rec(un):
+            n = len(srcs[un])
+            rc = small.tile([P, 4], F32, tag="rc", name="rc")
+            nc.vector.reciprocal(out=rc[:, 0:n], in_=st[("nn", un)][:, 0:n])
+            r2 = small.tile([P, 4], F32, tag="r2", name="r2")
+            nc.vector.scalar_tensor_tensor(
+                out=r2[:, 0:n],
+                in0=st[("ssum", un)][:, 0:n],
+                scalar=1.0 / EPS,
+                in1=rc[:, 0:n],
+                op0=ALU.mult,
+                op1=ALU.mult,
+            )
+            st[("r2", un)] = r2
+
+        def wt(un):
+            n = len(srcs[un])
+            if un == "x":
+                ww = const.tile([P, 1, D], F32, name="w64")
+            else:
+                ww = work.tile([P, 4, D], F32, tag="w", name="ww", bufs=4)
+            for a in range(n):
+                nc.vector.tensor_scalar(
+                    out=ww[:, a, :],
+                    in0=st[("tau", un)][:, a, :],
+                    scalar1=st[("r2", un)][:, a : a + 1],
+                    scalar2=(1.0 if a % 2 == 0 else -1.0),
+                    op0=ALU.mult,
+                    op1=ALU.mult,
+                )
+            st[("w", un)] = ww
+
+        def w_of(t):
+            if t == NT:
+                return st[("w", "x")][:, 0, :]
+            return st[("w", t // 4)][:, t % 4, :]
+
+        def etrans(g):
+            for j in range(4):
+                eb = psum.tile([P, 4, P], F32, tag="e%d" % j, name="eb", bufs=1)
+                for q in range(4):
+                    t = 4 * g + q
+                    nc.tensor.matmul(
+                        out=eb[:, q, :],
+                        lhsT=w_of(t)[:, j * P : (j + 1) * P],
+                        rhs=ident[:],
+                        is_transpose=True,
+                        start=True,
+                        stop=False,
+                    )
+                    nc.tensor.matmul(
+                        out=eb[:, q, :],
+                        lhsT=w_of(t + 1)[:, j * P : (j + 1) * P],
+                        rhs=ident[:],
+                        is_transpose=True,
+                        start=False,
+                        stop=True,
+                    )
+                st[("e", g, j)] = eb
+
+        def absacc(g, js):
+            for j in js:
+                junk = work.tile([P, D], F32, tag="junk", name="junk")
+                nc.scalar.activation(
+                    out=junk[:],
+                    in_=st[("e", g, j)][:].rearrange("p q r -> p (q r)"),
+                    func=ACT.Abs,
+                    accum_out=part[:, j, g : g + 1],
+                )
+
+        transposes("w")
+        copy_out("w")
+        quant("w")
+        transposes(0)
+        copy_out(0)
+        quant(0)
+        transposes(1)
+        mx(0, 0)
+        mx(0, 1)
+
+        for i in range(NG + 3):
+            if i + 1 < NG:
+                copy_out(i + 1)
+            if i < NG:
+                for a in range(4):
+                    if a >= 2:
+                        mx(i, a)
+                    p1(i, a)
+                    p2(i, a)
+            if i == XI + 1:
+                mx("x", 0)
+                p1("x", 0)
+                p2("x", 0)
+            if i == XI:
+                transposes("x")
+            if 0 <= i - 3 < NG:
+                etrans(i - 3)
+            if i == XI:
+                copy_out("x")
+            if i + 1 < NG:
+                quant(i + 1)
+            if i == XI:
+                quant("x")
+            if i < NG:
+                tau(i)
+                m2(i)
+            if i == XI + 1:
+                tau("x")
+                m2("x")
+            if 0 <= i - 3 < NG:
+                absacc(i - 3, [0, 1])
+            if 0 <= i - 1 < NG:
+                wt(i - 1)
+            if i == XI + 2:
+                wt("x")
+            if i < NG:
+                root(i)
+            if i == XI + 1:
+                root("x")
+            if 0 <= i - 3 < NG:
+                absacc(i - 3, [2, 3])
+            if i < NG:
+                rec(i)
+            if i == XI + 1:
+                rec("x")
+            if i + 2 < NG:
+                transposes(i + 2)
+            if i + 1 < NG:
+                mx(i + 1, 0)
+                mx(i + 1, 1)
+
+        dcol = small.tile([P, 4], F32, tag="dcol", name="dcol")
+        nc.vector.tensor_reduce(out=dcol[:], in_=part[:], axis=AX.X, op=ALU.add)
+        fin = psum.tile([P, D], F32, tag="acc", name="fin")
+        for j in range(4):
+            nc.tensor.matmul(
+                out=fin[:, j * P : (j + 1) * P],
+                lhsT=dcol[:, j : j + 1].to_broadcast([P, P]),
+                rhs=ident[:],
+                start=True,
+                stop=True,
+            )
+        res = const.tile([P, D], F32, name="res")
+        nc.vector.tensor_copy(out=res[:], in_=fin[:])
+        for a in range(4):
+            eng = nc.sync if a % 2 == 0 else nc.scalar
+            eng.dma_start(out=out[a * P : (a + 1) * P, :], in_=res[:])

@@ -21,7 +21,6 @@ NT = 64
 NG = 16
 EPS = 1e-8
 DELTA = EPS / math.sqrt(D)
-XI = 8
 
 
 def tile_dispatcher_pa_kernel(tc, inv, Wk, bk, out):
@@ -29,272 +28,237 @@ def tile_dispatcher_pa_kernel(tc, inv, Wk, bk, out):
     rows = inv.flatten_outer_dims().rearrange("(p t) k -> p t k", t=NT)
     with ExitStack() as ctx:
         const = ctx.enter_context(tc.tile_pool(name="const", bufs=1))
-        work = ctx.enter_context(tc.tile_pool(name="work", bufs=2))
-        small = ctx.enter_context(tc.tile_pool(name="small", bufs=4))
+        work = ctx.enter_context(tc.tile_pool(name="work", bufs=3))
+        small = ctx.enter_context(tc.tile_pool(name="small", bufs=3))
         psum = ctx.enter_context(tc.psum_pool(name="psum", bufs=2))
+        ctx.enter_context(tc.manual_schedule())
 
+        b_bf = const.tile([P, D], BF16, name="b_bf")
+        nc.scalar.dma_start(out=b_bf[:], in_=bk.partition_broadcast(P))
+        w_sb = const.tile([P, 4, D], BF16, name="w_sb")
+        nc.sync.dma_start(out=w_sb[:], in_=Wk.rearrange("(a p) k -> p a k", p=P))
+        xs = []
+        for g in range(NG):
+            xg = const.tile([P, 4, D], BF16, name="x%d" % g)
+            nc.sync.dma_start(out=xg[:], in_=rows[:, 4 * g : 4 * g + 4, :])
+            xs.append(xg)
         one = const.tile([P, 1], F32, name="one")
         nc.vector.memset(one[:], 1.0)
         warm = const.tile([P, 1], F32, name="warm")
         nc.scalar.activation(out=warm[:], in_=one[:], func=ACT.Sqrt)
         ident = const.tile([P, P], F32, name="ident")
         make_identity(nc, ident[:])
-
-        w_sb = const.tile([P, 4, D], BF16, name="w_sb")
-        nc.sync.dma_start(out=w_sb[:], in_=Wk.rearrange("(a p) k -> p a k", p=P))
-        b_bf = const.tile([P, D], BF16, name="b_bf")
-        nc.scalar.dma_start(out=b_bf[:], in_=bk.partition_broadcast(P))
-        xs = []
-        for g in range(NG):
-            xg = const.tile([P, 4, D], BF16, name="x%d" % g)
-            nc.sync.dma_start(out=xg[:], in_=rows[:, 4 * g : 4 * g + 4, :])
-            xs.append(xg)
-        x64 = const.tile([P, D], BF16, name="x64")
-        nc.sync.dma_start(out=x64[0 : P - 1, :], in_=rows[1:P, 0, :])
-        nc.sync.dma_start(out=x64[P - 1 : P, :], in_=rows[P - 1 : P, NT - 1, :])
+        shift = const.tile([P, P], F32, name="shift")
+        nc.vector.tensor_copy(out=shift[:, 1:P], in_=ident[:, 0 : P - 1])
+        nc.vector.tensor_copy(out=shift[:, 0:1], in_=ident[:, P - 1 : P])
         bias = const.tile([P, D], F32, name="bias")
-        nc.vector.tensor_copy(out=bias[:], in_=b_bf[:])
-        part = const.tile([P, 4, NG], F32, name="part")
-
-        srcs = {"w": [w_sb[:, a, :] for a in range(4)], "x": [x64[:, :]]}
-        for g in range(NG):
-            srcs[g] = [xs[g][:, a, :] for a in range(4)]
+        part = const.tile([P, 4, NG + 1], F32, name="part")
+        w_first = const.tile([P, D], F32, name="w_first")
+        w_codes = const.tile([P, D], U32, name="w_codes", align_bytes=64)
+        w_scl = const.tile([P, D], U8, name="w_scl", align_bytes=64)
         st = {}
 
-        def transposes(un):
-            n = len(srcs[un])
-            banks = []
-            for h0 in range(0, n, 2):
+        def ok(g):
+            return 0 <= g < NG
+
+        def flip(bank, srcs):
+            for h in range(2):
+                words = srcs[h].bitcast(F32)
+                for u in range(2):
+                    nc.tensor.transpose(bank[:, h, u, :], words[:, u * P : (u + 1) * P], ident[:])
+
+        def t1(g, h):
+            if ok(g):
                 xt = psum.tile([P, 2, 2, P], F32, tag="xt", name="xt")
-                for h in range(min(2, n - h0)):
-                    words = srcs[un][h0 + h].bitcast(F32)
-                    for u in range(2):
-                        nc.tensor.transpose(xt[:, h, u, :], words[:, u * P : (u + 1) * P], ident[:])
-                banks.append(xt)
-            st[("xt", un)] = banks
+                flip(xt, [xs[g][:, 2 * h, :], xs[g][:, 2 * h + 1, :]])
+                st[("xt", g, h)] = xt
 
-        def copy_out(un):
-            n = len(srcs[un])
-            grp = work.tile([P, 4 * D], BF16, tag="grp", name="grp", align_bytes=64)
-            gv = grp[:].bitcast(F32).rearrange("p (a r u) -> p a r u", a=4, r=P, u=2)
-            for b, xt in enumerate(st[("xt", un)]):
-                m = min(2, n - 2 * b)
+        def cp(g, h):
+            if ok(g):
+                grp = work.tile([P, 2 * D], BF16, tag="grp", name="grp", align_bytes=64)
                 nc.scalar.copy(
-                    out=gv[:, 2 * b : 2 * b + m, :, :],
-                    in_=xt[:, 0:m, :, :].rearrange("p h u r -> p h r u"),
+                    out=grp[:].bitcast(F32).rearrange("p (a r u) -> p a r u", a=2, r=P, u=2),
+                    in_=st[("xt", g, h)][:].rearrange("p h u r -> p h r u"),
                 )
-            st[("grp", un)] = grp
+                st[("grp", g, h)] = grp
 
-        def quant(un):
-            n = len(srcs[un])
-            if un == "w":
-                codes = const.tile([P, D], U32, name="w_codes", align_bytes=64)
-                scl = const.tile([P, D], U8, name="w_scl", align_bytes=64)
-            else:
-                codes = work.tile([P, D], U32, tag="codes", name="codes", align_bytes=64)
-                scl = work.tile([P, D], U8, tag="scl", name="scl", align_bytes=64)
-            nc.vector.quantize_mx(
-                out=codes[:, 0 : n * P].bitcast(FP8X4),
-                scales=scl[:, 0 : n * P],
-                in_=st[("grp", un)][:, 0 : n * D],
-            )
-            st[("codes", un)] = codes
-            st[("scl", un)] = scl
+        def qz(g, h):
+            if ok(g):
+                codes = work.tile([P, 2 * P], U32, tag="codes", name="codes", align_bytes=64)
+                scl = work.tile([P, 2 * P], U8, tag="scl", name="scl", align_bytes=64)
+                nc.vector.quantize_mx(out=codes[:].bitcast(FP8X4), scales=scl[:], in_=st[("grp", g, h)][:])
+                st[("codes", g, h)] = codes
+                st[("scl", g, h)] = scl
 
-        def mx(un, a):
-            acc = psum.tile([P, D], F32, tag="acc", name="acc")
-            nc.tensor.matmul_mx(
-                out=acc[:],
-                lhsT=st[("codes", un)][:, a * P : (a + 1) * P].bitcast(FP8X4),
-                lhsT_scale=st[("scl", un)][:, a * P : (a + 1) * P],
-                rhs=st[("codes", "w")][:].bitcast(FP8X4),
-                rhs_scale=st[("scl", "w")][:],
-                start=True,
-                stop=True,
-            )
-            st[("acc", un, a)] = acc
+        def mx(g, a):
+            if ok(g):
+                acc = psum.tile([P, D], F32, tag="acc", name="acc")
+                c0 = (a % 2) * P
+                nc.tensor.matmul_mx(
+                    out=acc[:],
+                    lhsT=st[("codes", g, a // 2)][:, c0 : c0 + P].bitcast(FP8X4),
+                    lhsT_scale=st[("scl", g, a // 2)][:, c0 : c0 + P],
+                    rhs=w_codes[:].bitcast(FP8X4),
+                    rhs_scale=w_scl[:],
+                    start=True,
+                    stop=True,
+                )
+                st[("acc", g, a)] = acc
 
-        def p1(un, a):
-            if a == 0:
-                st[("o", un)] = work.tile([P, 4, D], F32, tag="o", name="o")
-                st[("ssum", un)] = small.tile([P, 4], F32, tag="ssum", name="ssum")
-                st[("n2", un)] = small.tile([P, 4], F32, tag="n2", name="n2")
-            nc.vector.scalar_tensor_tensor(
-                out=st[("o", un)][:, a, :],
-                in0=st[("acc", un, a)][:],
-                scalar=1.0,
-                in1=bias[:],
-                op0=ALU.mult,
-                op1=ALU.add,
-                accum_out=st[("ssum", un)][:, a : a + 1],
-            )
+        def p1(g, a):
+            if ok(g):
+                if a == 0:
+                    st[("ssum", g)] = small.tile([P, 4], F32, tag="ssum", name="ssum")
+                    st[("n2", g)] = small.tile([P, 4], F32, tag="n2", name="n2")
+                if a % 2 == 0:
+                    st[("o", g, a // 2)] = work.tile([P, 2, D], F32, tag="o", name="o")
+                nc.vector.scalar_tensor_tensor(
+                    out=st[("o", g, a // 2)][:, a % 2, :],
+                    in0=st[("acc", g, a)][:],
+                    scalar=1.0,
+                    in1=bias[:],
+                    op0=ALU.mult,
+                    op1=ALU.add,
+                    accum_out=st[("ssum", g)][:, a : a + 1],
+                )
 
-        def p2(un, a):
-            junk = work.tile([P, D], F32, tag="junk", name="junk")
-            nc.scalar.activation(
-                out=junk[:],
-                in_=st[("o", un)][:, a, :],
-                func=ACT.Square,
-                accum_out=st[("n2", un)][:, a : a + 1],
-            )
+        def p2(g, a):
+            if ok(g):
+                junk = work.tile([P, D], F32, tag="junk", name="junk")
+                nc.scalar.activation(
+                    out=junk[:],
+                    in_=st[("o", g, a // 2)][:, a % 2, :],
+                    func=ACT.Square,
+                    accum_out=st[("n2", g)][:, a : a + 1],
+                )
 
-        def tau(un):
-            n = len(srcs[un])
-            tt = work.tile([P, 4, D], F32, tag="tau", name="tt")
-            nc.vector.tensor_scalar(
-                out=tt[:, 0:n, :],
-                in0=st[("o", un)][:, 0:n, :],
-                scalar1=DELTA,
-                scalar2=-DELTA,
-                op0=ALU.min,
-                op1=ALU.max,
-            )
-            st[("tau", un)] = tt
-
-        def m2(un):
-            n = len(srcs[un])
-            mm = small.tile([P, 4], F32, tag="m2", name="mm")
-            nc.vector.tensor_scalar(
-                out=mm[:, 0:n], in0=st[("n2", un)][:, 0:n], scalar1=EPS * EPS, scalar2=None, op0=ALU.max
-            )
-            st[("m2", un)] = mm
-
-        def root(un):
-            n = len(srcs[un])
-            nn = small.tile([P, 4], F32, tag="nn", name="nn")
-            nc.scalar.activation(out=nn[:, 0:n], in_=st[("m2", un)][:, 0:n], func=ACT.Sqrt)
-            st[("nn", un)] = nn
-
-        def rec(un):
-            n = len(srcs[un])
-            rc = small.tile([P, 4], F32, tag="rc", name="rc")
-            nc.vector.reciprocal(out=rc[:, 0:n], in_=st[("nn", un)][:, 0:n])
-            r2 = small.tile([P, 4], F32, tag="r2", name="r2")
-            nc.vector.scalar_tensor_tensor(
-                out=r2[:, 0:n],
-                in0=st[("ssum", un)][:, 0:n],
-                scalar=1.0 / EPS,
-                in1=rc[:, 0:n],
-                op0=ALU.mult,
-                op1=ALU.mult,
-            )
-            st[("r2", un)] = r2
-
-        def wt(un):
-            n = len(srcs[un])
-            if un == "x":
-                ww = const.tile([P, 1, D], F32, name="w64")
-            else:
-                ww = work.tile([P, 4, D], F32, tag="w", name="ww", bufs=4)
-            for a in range(n):
+        def tau(g, h):
+            if ok(g):
+                tt = work.tile([P, 2, D], F32, tag="tau", name="tt", bufs=4)
                 nc.vector.tensor_scalar(
-                    out=ww[:, a, :],
-                    in0=st[("tau", un)][:, a, :],
-                    scalar1=st[("r2", un)][:, a : a + 1],
+                    out=tt[:], in0=st[("o", g, h)][:], scalar1=DELTA, scalar2=-DELTA, op0=ALU.min, op1=ALU.max
+                )
+                st[("tau", g, h)] = tt
+
+        def m2(g):
+            if ok(g):
+                mm = small.tile([P, 4], F32, tag="m2", name="mm")
+                nc.vector.tensor_scalar(
+                    out=mm[:], in0=st[("n2", g)][:], scalar1=EPS * EPS, scalar2=None, op0=ALU.max
+                )
+                st[("m2", g)] = mm
+
+        def root(g):
+            if ok(g):
+                nn = small.tile([P, 4], F32, tag="nn", name="nn")
+                nc.scalar.activation(out=nn[:], in_=st[("m2", g)][:], func=ACT.Sqrt)
+                st[("nn", g)] = nn
+
+        def rec(g):
+            if ok(g):
+                rc = small.tile([P, 4], F32, tag="rc", name="rc")
+                nc.vector.reciprocal(out=rc[:], in_=st[("nn", g)][:])
+                r2 = small.tile([P, 4], F32, tag="r2", name="r2")
+                nc.vector.scalar_tensor_tensor(
+                    out=r2[:], in0=st[("ssum", g)][:], scalar=1.0 / EPS, in1=rc[:], op0=ALU.mult, op1=ALU.mult
+                )
+                st[("r2", g)] = r2
+
+        def wt(g, a):
+            if ok(g):
+                if g == 0 and a == 0:
+                    ww = w_first
+                else:
+                    ww = work.tile([P, D], F32, tag="w", name="ww", bufs=12)
+                nc.vector.tensor_scalar(
+                    out=ww[:],
+                    in0=st[("tau", g, a // 2)][:, a % 2, :],
+                    scalar1=st[("r2", g)][:, a : a + 1],
                     scalar2=(1.0 if a % 2 == 0 else -1.0),
                     op0=ALU.mult,
                     op1=ALU.mult,
                 )
-            st[("w", un)] = ww
+                st[("w", 4 * g + a)] = ww
 
-        def w_of(t):
-            if t == NT:
-                return st[("w", "x")][:, 0, :]
-            return st[("w", t // 4)][:, t % 4, :]
+        def add_flipped(dst, first, second, perm, j):
+            nc.tensor.matmul(
+                out=dst, lhsT=first[:, j * P : (j + 1) * P], rhs=ident[:], is_transpose=True, start=True, stop=False
+            )
+            nc.tensor.matmul(
+                out=dst, lhsT=second[:, j * P : (j + 1) * P], rhs=perm[:], is_transpose=True, start=False, stop=True
+            )
 
-        def etrans(g):
-            for j in range(4):
+        def ed(g, j):
+            if 0 <= g <= NG:
                 eb = psum.tile([P, 4, P], F32, tag="e%d" % j, name="eb", bufs=1)
-                for q in range(4):
-                    t = 4 * g + q
-                    nc.tensor.matmul(
-                        out=eb[:, q, :],
-                        lhsT=w_of(t)[:, j * P : (j + 1) * P],
-                        rhs=ident[:],
-                        is_transpose=True,
-                        start=True,
-                        stop=False,
-                    )
-                    nc.tensor.matmul(
-                        out=eb[:, q, :],
-                        lhsT=w_of(t + 1)[:, j * P : (j + 1) * P],
-                        rhs=ident[:],
-                        is_transpose=True,
-                        start=False,
-                        stop=True,
-                    )
+                if g == NG:
+                    add_flipped(eb[:, 0, :], st[("w", 0)], st[("w", NT - 1)], shift, j)
+                else:
+                    for q in range(4):
+                        if 4 * g + q >= 1:
+                            add_flipped(eb[:, q, :], st[("w", 4 * g + q - 1)], st[("w", 4 * g + q)], ident, j)
                 st[("e", g, j)] = eb
 
-        def absacc(g, js):
-            for j in js:
+        def ab(g, j):
+            if 0 <= g <= NG:
+                flat = st[("e", g, j)][:].rearrange("p q r -> p (q r)")
+                lo, hi = 0, D
+                if g == 0:
+                    lo = P
+                if g == NG:
+                    lo, hi = 1, P
                 junk = work.tile([P, D], F32, tag="junk", name="junk")
                 nc.scalar.activation(
-                    out=junk[:],
-                    in_=st[("e", g, j)][:].rearrange("p q r -> p (q r)"),
-                    func=ACT.Abs,
-                    accum_out=part[:, j, g : g + 1],
+                    out=junk[:, lo:hi], in_=flat[:, lo:hi], func=ACT.Abs, accum_out=part[:, j, g : g + 1]
                 )
 
-        transposes("w")
-        copy_out("w")
-        quant("w")
-        transposes(0)
-        copy_out(0)
-        quant(0)
-        transposes(1)
-        mx(0, 0)
-        mx(0, 1)
+        grp_w = const.tile([P, 4 * D], BF16, name="grp_w", align_bytes=64)
+        for h in range(2):
+            wb = psum.tile([P, 2, 2, P], F32, tag="e%d" % h, name="wb", bufs=1)
+            flip(wb, [w_sb[:, 2 * h, :], w_sb[:, 2 * h + 1, :]])
+            nc.vector.tensor_copy(
+                out=grp_w[:, 2 * h * D : (2 * h + 2) * D].bitcast(F32).rearrange("p (a r u) -> p a r u", a=2, r=P, u=2),
+                in_=wb[:].rearrange("p h u r -> p h r u"),
+            )
+        nc.vector.quantize_mx(out=w_codes[:].bitcast(FP8X4), scales=w_scl[:], in_=grp_w[:])
+        nc.vector.tensor_copy(out=bias[:], in_=b_bf[:])
 
-        for i in range(NG + 3):
-            if i + 1 < NG:
-                copy_out(i + 1)
-            if i < NG:
-                for a in range(4):
-                    if a >= 2:
-                        mx(i, a)
-                    p1(i, a)
-                    p2(i, a)
-            if i == XI + 1:
-                mx("x", 0)
-                p1("x", 0)
-                p2("x", 0)
-            if i == XI:
-                transposes("x")
-            if 0 <= i - 3 < NG:
-                etrans(i - 3)
-            if i == XI:
-                copy_out("x")
-            if i + 1 < NG:
-                quant(i + 1)
-            if i == XI:
-                quant("x")
-            if i < NG:
-                tau(i)
-                m2(i)
-            if i == XI + 1:
-                tau("x")
-                m2("x")
-            if 0 <= i - 3 < NG:
-                absacc(i - 3, [0, 1])
-            if 0 <= i - 1 < NG:
-                wt(i - 1)
-            if i == XI + 2:
-                wt("x")
-            if i < NG:
-                root(i)
-            if i == XI + 1:
-                root("x")
-            if 0 <= i - 3 < NG:
-                absacc(i - 3, [2, 3])
-            if i < NG:
-                rec(i)
-            if i == XI + 1:
-                rec("x")
-            if i + 2 < NG:
-                transposes(i + 2)
-            if i + 1 < NG:
-                mx(i + 1, 0)
-                mx(i + 1, 1)
+        for i in range(-2, NG + 4):
+            ed(i - 2, 0)
+            ab(i - 3, 3)
+            p1(i, 0)
+            m2(i - 1)
+            mx(i, 2)
+            p2(i, 0)
+            root(i - 1)
+            qz(i + 1, 0)
+            ed(i - 2, 1)
+            t1(i + 1, 1)
+            ab(i - 2, 0)
+            p1(i, 1)
+            mx(i, 3)
+            p2(i, 1)
+            tau(i, 0)
+            rec(i - 1)
+            cp(i + 1, 1)
+            ed(i - 2, 2)
+            t1(i + 2, 0)
+            ab(i - 2, 1)
+            p1(i, 2)
+            p2(i, 2)
+            wt(i - 1, 0)
+            wt(i - 1, 1)
+            cp(i + 2, 0)
+            ed(i - 2, 3)
+            ab(i - 2, 2)
+            p1(i, 3)
+            mx(i + 1, 0)
+            mx(i + 1, 1)
+            p2(i, 3)
+            wt(i - 1, 2)
+            wt(i - 1, 3)
+            tau(i, 1)
+            qz(i + 1, 1)
 
         dcol = small.tile([P, 4], F32, tag="dcol", name="dcol")
         nc.vector.tensor_reduce(out=dcol[:], in_=part[:], axis=AX.X, op=ALU.add)

@@ -21,6 +21,7 @@ NT = 64
 NG = 16
 EPS = 1e-8
 DELTA = EPS / math.sqrt(D)
+PLAIN_BANKS = (0, 3)
 
 
 def tile_dispatcher_pa_kernel(tc, inv, Wk, bk, out):
@@ -180,9 +181,14 @@ def tile_dispatcher_pa_kernel(tc, inv, Wk, bk, out):
                 )
                 st[("w", 4 * g + a)] = ww
 
-        def add_flipped(dst, first, second, perm, j):
+        def add_flipped(dst, first, second, perm, j, plain):
             nc.tensor.matmul(
-                out=dst, lhsT=first[:, j * P : (j + 1) * P], rhs=ident[:], is_transpose=True, start=True, stop=False
+                out=dst,
+                lhsT=first[:, j * P : (j + 1) * P],
+                rhs=ident[:],
+                is_transpose=(not plain),
+                start=True,
+                stop=False,
             )
             nc.tensor.matmul(
                 out=dst, lhsT=second[:, j * P : (j + 1) * P], rhs=perm[:], is_transpose=True, start=False, stop=True
@@ -192,11 +198,13 @@ def tile_dispatcher_pa_kernel(tc, inv, Wk, bk, out):
             if 0 <= g <= NG:
                 eb = psum.tile([P, 4, P], F32, tag="e%d" % j, name="eb", bufs=1)
                 if g == NG:
-                    add_flipped(eb[:, 0, :], st[("w", 0)], st[("w", NT - 1)], shift, j)
+                    add_flipped(eb[:, 0, :], st[("w", 0)], st[("w", NT - 1)], shift, j, j in PLAIN_BANKS)
                 else:
                     for q in range(4):
                         if 4 * g + q >= 1:
-                            add_flipped(eb[:, q, :], st[("w", 4 * g + q - 1)], st[("w", 4 * g + q)], ident, j)
+                            add_flipped(
+                                eb[:, q, :], st[("w", 4 * g + q - 1)], st[("w", 4 * g + q)], ident, j, q == 1 and j in PLAIN_BANKS
+                            )
                 st[("e", g, j)] = eb
 
         def ab(g, j):

@@ -37,11 +37,17 @@ def tile_dispatcher_pa_kernel(tc, inv, Wk, bk, out):
         b_bf = const.tile([P, D], BF16, name="b_bf")
         nc.scalar.dma_start(out=b_bf[:], in_=bk.partition_broadcast(P))
         w_sb = const.tile([P, 4, D], BF16, name="w_sb")
-        nc.sync.dma_start(out=w_sb[:], in_=Wk.rearrange("(a p) k -> p a k", p=P))
+        w_rows = Wk.rearrange("(a p) k -> p a k", p=P)
+        for h in range(2):
+            nc.sync.dma_start(out=w_sb[:, 2 * h : 2 * h + 2, :], in_=w_rows[:, 2 * h : 2 * h + 2, :])
         xs = []
         for g in range(NG):
             xg = const.tile([P, 4, D], BF16, name="x%d" % g)
-            nc.sync.dma_start(out=xg[:], in_=rows[:, 4 * g : 4 * g + 4, :])
+            if g == 0:
+                for h in range(2):
+                    nc.sync.dma_start(out=xg[:, 2 * h : 2 * h + 2, :], in_=rows[:, 2 * h : 2 * h + 2, :])
+            else:
+                nc.sync.dma_start(out=xg[:], in_=rows[:, 4 * g : 4 * g + 4, :])
             xs.append(xg)
         one = const.tile([P, 1], F32, name="one")
         nc.vector.memset(one[:], 1.0)
@@ -77,10 +83,12 @@ def tile_dispatcher_pa_kernel(tc, inv, Wk, bk, out):
         def cp(g, h):
             if ok(g):
                 grp = work.tile([P, 2 * D], BF16, tag="grp", name="grp", align_bytes=64)
-                nc.scalar.copy(
-                    out=grp[:].bitcast(F32).rearrange("p (a r u) -> p a r u", a=2, r=P, u=2),
-                    in_=st[("xt", g, h)][:].rearrange("p h u r -> p h r u"),
-                )
+                dst = grp[:].bitcast(F32).rearrange("p (a r u) -> p a r u", a=2, r=P, u=2)
+                src = st[("xt", g, h)][:].rearrange("p h u r -> p h r u")
+                if h == 0:
+                    nc.scalar.copy(out=dst, in_=src)
+                else:
+                    nc.vector.tensor_copy(out=dst, in_=src)
                 st[("grp", g, h)] = grp
 
         def qz(g, h):
@@ -136,7 +144,7 @@ def tile_dispatcher_pa_kernel(tc, inv, Wk, bk, out):
         def tau(g, h):
             if ok(g):
                 tt = work.tile([P, 2, D], F32, tag="tau", name="tt", bufs=4)
-                nc.vector.tensor_scalar(
+                nc.gpsimd.tensor_scalar(
                     out=tt[:], in0=st[("o", g, h)][:], scalar1=DELTA, scalar2=-DELTA, op0=ALU.min, op1=ALU.max
                 )
                 st[("tau", g, h)] = tt
@@ -232,41 +240,41 @@ def tile_dispatcher_pa_kernel(tc, inv, Wk, bk, out):
         nc.vector.tensor_copy(out=bias[:], in_=b_bf[:])
 
         for i in range(-2, NG + 4):
+            tau(i - 1, 1)
             ed(i - 2, 0)
-            ab(i - 3, 3)
+            ab(i - 3, 2)
             p1(i, 0)
-            m2(i - 1)
             mx(i, 2)
             p2(i, 0)
-            root(i - 1)
-            qz(i + 1, 0)
-            ed(i - 2, 1)
-            t1(i + 1, 1)
-            ab(i - 2, 0)
             p1(i, 1)
+            t1(i + 1, 1)
+            ed(i - 2, 1)
             mx(i, 3)
+            ab(i - 3, 3)
             p2(i, 1)
-            tau(i, 0)
             rec(i - 1)
-            cp(i + 1, 1)
-            ed(i - 2, 2)
-            t1(i + 2, 0)
-            ab(i - 2, 1)
-            p1(i, 2)
-            p2(i, 2)
             wt(i - 1, 0)
             wt(i - 1, 1)
-            cp(i + 2, 0)
-            ed(i - 2, 3)
-            ab(i - 2, 2)
+            qz(i + 1, 0)
+            tau(i, 0)
+            ed(i - 2, 2)
+            t1(i + 2, 0)
+            ab(i - 2, 0)
+            p1(i, 2)
+            p2(i, 2)
+            cp(i + 1, 1)
             p1(i, 3)
+            ed(i - 2, 3)
+            ab(i - 2, 1)
+            p2(i, 3)
             mx(i + 1, 0)
             mx(i + 1, 1)
-            p2(i, 3)
+            cp(i + 2, 0)
             wt(i - 1, 2)
             wt(i - 1, 3)
-            tau(i, 1)
             qz(i + 1, 1)
+            m2(i)
+            root(i)
 
         dcol = small.tile([P, 4], F32, tag="dcol", name="dcol")
         nc.vector.tensor_reduce(out=dcol[:], in_=part[:], axis=AX.X, op=ALU.add)

@@ -21,7 +21,6 @@ NT = 64
 NG = 16
 EPS = 1e-8
 DELTA = EPS / math.sqrt(D)
-PLAIN_BANKS = (0, 3)
 
 
 def tile_dispatcher_pa_kernel(tc, inv, Wk, bk, out):
@@ -83,12 +82,10 @@ def tile_dispatcher_pa_kernel(tc, inv, Wk, bk, out):
         def cp(g, h):
             if ok(g):
                 grp = work.tile([P, 2 * D], BF16, tag="grp", name="grp", align_bytes=64)
-                dst = grp[:].bitcast(F32).rearrange("p (a r u) -> p a r u", a=2, r=P, u=2)
-                src = st[("xt", g, h)][:].rearrange("p h u r -> p h r u")
-                if h == 0:
-                    nc.scalar.copy(out=dst, in_=src)
-                else:
-                    nc.vector.tensor_copy(out=dst, in_=src)
+                nc.scalar.copy(
+                    out=grp[:].bitcast(F32).rearrange("p (a r u) -> p a r u", a=2, r=P, u=2),
+                    in_=st[("xt", g, h)][:].rearrange("p h u r -> p h r u"),
+                )
                 st[("grp", g, h)] = grp
 
         def qz(g, h):
@@ -144,7 +141,7 @@ def tile_dispatcher_pa_kernel(tc, inv, Wk, bk, out):
         def tau(g, h):
             if ok(g):
                 tt = work.tile([P, 2, D], F32, tag="tau", name="tt", bufs=4)
-                nc.gpsimd.tensor_scalar(
+                nc.vector.tensor_scalar(
                     out=tt[:], in0=st[("o", g, h)][:], scalar1=DELTA, scalar2=-DELTA, op0=ALU.min, op1=ALU.max
                 )
                 st[("tau", g, h)] = tt
@@ -206,12 +203,12 @@ def tile_dispatcher_pa_kernel(tc, inv, Wk, bk, out):
             if 0 <= g <= NG:
                 eb = psum.tile([P, 4, P], F32, tag="e%d" % j, name="eb", bufs=1)
                 if g == NG:
-                    add_flipped(eb[:, 0, :], st[("w", 0)], st[("w", NT - 1)], shift, j, j in PLAIN_BANKS)
+                    add_flipped(eb[:, 0, :], st[("w", 0)], st[("w", NT - 1)], shift, j, False)
                 else:
                     for q in range(4):
                         if 4 * g + q >= 1:
                             add_flipped(
-                                eb[:, q, :], st[("w", 4 * g + q - 1)], st[("w", 4 * g + q)], ident, j, q == 1 and j in PLAIN_BANKS
+                                eb[:, q, :], st[("w", 4 * g + q - 1)], st[("w", 4 * g + q)], ident, j, q == 1
                             )
                 st[("e", g, j)] = eb
 
@@ -240,53 +237,47 @@ def tile_dispatcher_pa_kernel(tc, inv, Wk, bk, out):
         nc.vector.tensor_copy(out=bias[:], in_=b_bf[:])
 
         for i in range(-2, NG + 4):
-            tau(i - 1, 1)
             ed(i - 2, 0)
-            ab(i - 3, 2)
+            ab(i - 3, 3)
             p1(i, 0)
+            m2(i - 1)
             mx(i, 2)
             p2(i, 0)
-            p1(i, 1)
-            t1(i + 1, 1)
-            ed(i - 2, 1)
-            mx(i, 3)
-            ab(i - 3, 3)
-            p2(i, 1)
-            rec(i - 1)
-            wt(i - 1, 0)
-            wt(i - 1, 1)
+            root(i - 1)
             qz(i + 1, 0)
+            ed(i - 2, 1)
+            t1(i + 1, 1)
+            ab(i - 2, 0)
+            p1(i, 1)
+            mx(i, 3)
+            p2(i, 1)
             tau(i, 0)
+            rec(i - 1)
+            cp(i + 1, 1)
             ed(i - 2, 2)
             t1(i + 2, 0)
-            ab(i - 2, 0)
+            ab(i - 2, 1)
             p1(i, 2)
             p2(i, 2)
-            cp(i + 1, 1)
-            p1(i, 3)
+            wt(i - 1, 0)
+            wt(i - 1, 1)
+            cp(i + 2, 0)
             ed(i - 2, 3)
-            ab(i - 2, 1)
-            p2(i, 3)
+            p1(i, 3)
             mx(i + 1, 0)
             mx(i + 1, 1)
-            cp(i + 2, 0)
+            p2(i, 3)
+            ab(i - 2, 2)
             wt(i - 1, 2)
             wt(i - 1, 3)
+            tau(i, 1)
             qz(i + 1, 1)
-            m2(i)
-            root(i)
 
         dcol = small.tile([P, 4], F32, tag="dcol", name="dcol")
         nc.vector.tensor_reduce(out=dcol[:], in_=part[:], axis=AX.X, op=ALU.add)
         fin = psum.tile([P, D], F32, tag="acc", name="fin")
         for j in range(4):
-            nc.tensor.matmul(
-                out=fin[:, j * P : (j + 1) * P],
-                lhsT=dcol[:, j : j + 1].to_broadcast([P, P]),
-                rhs=ident[:],
-                start=True,
-                stop=True,
-            )
+            nc.tensor.transpose(fin[:, j * P : (j + 1) * P], dcol[:, j : j + 1].to_broadcast([P, P]), ident[:])
         res = const.tile([P, D], F32, name="res")
         nc.vector.tensor_copy(out=res[:], in_=fin[:])
         for a in range(4):

@@ -186,30 +186,28 @@ def tile_dispatcher_pa_kernel(tc, inv, Wk, bk, out):
                 )
                 st[("w", 4 * g + a)] = ww
 
-        def add_flipped(dst, first, second, perm, j, plain):
+        def flip_w(dst, node, perm, j, plain, first, last):
             nc.tensor.matmul(
                 out=dst,
-                lhsT=first[:, j * P : (j + 1) * P],
-                rhs=ident[:],
+                lhsT=st[("w", node)][:, j * P : (j + 1) * P],
+                rhs=perm[:],
                 is_transpose=(not plain),
-                start=True,
-                stop=False,
-            )
-            nc.tensor.matmul(
-                out=dst, lhsT=second[:, j * P : (j + 1) * P], rhs=perm[:], is_transpose=True, start=False, stop=True
+                start=first,
+                stop=last,
             )
 
         def ed(g, j):
             if 0 <= g <= NG:
                 eb = psum.tile([P, 4, P], F32, tag="e%d" % j, name="eb", bufs=1)
                 if g == NG:
-                    add_flipped(eb[:, 0, :], st[("w", 0)], st[("w", NT - 1)], shift, j, False)
+                    flip_w(eb[:, 0, :], 0, ident, j, False, True, False)
+                    flip_w(eb[:, 0, :], NT - 1, shift, j, False, False, True)
                 else:
-                    for q in range(4):
-                        if 4 * g + q >= 1:
-                            add_flipped(
-                                eb[:, q, :], st[("w", 4 * g + q - 1)], st[("w", 4 * g + q)], ident, j, q == 1
-                            )
+                    qs = [q for q in range(4) if 4 * g + q >= 1]
+                    for q in qs:
+                        flip_w(eb[:, q, :], 4 * g + q - 1, ident, j, q == 1, q == qs[0], False)
+                    for q in qs:
+                        flip_w(eb[:, q, :], 4 * g + q, ident, j, False, False, q == 3)
                 st[("e", g, j)] = eb
 
         def ab(g, j):

import math
from contextlib import ExitStack

import concourse.mybir as mybir
from concourse.masks import make_identity

FLOPS = 2 * 8192 * 512 * 512

F32 = mybir.dt.float32
BF16 = mybir.dt.bfloat16
U32 = mybir.dt.uint32
U8 = mybir.dt.uint8
FP8X4 = mybir.dt.float8_e4m3fn_x4
ALU = mybir.AluOpType
ACT = mybir.ActivationFunctionType
AX = mybir.AxisListType

P = 128
D = 512
NT = 64
NG = 16
EPS = 1e-8
DELTA = EPS / math.sqrt(D)


def tile_dispatcher_pa_kernel(tc, inv, Wk, bk, out):
    nc = tc.nc
    rows = inv.flatten_outer_dims().rearrange("(p t) k -> p t k", t=NT)
    with ExitStack() as ctx:
        const = ctx.enter_context(tc.tile_pool(name="const", bufs=1))
        work = ctx.enter_context(tc.tile_pool(name="work", bufs=3))
        small = ctx.enter_context(tc.tile_pool(name="small", bufs=3))
        psum = ctx.enter_context(tc.psum_pool(name="psum", bufs=2))
        ctx.enter_context(tc.manual_schedule())

        b_bf = const.tile([P, D], BF16, name="b_bf")
        nc.scalar.dma_start(out=b_bf[:], in_=bk.partition_broadcast(P))
        w_sb = const.tile([P, 4, D], BF16, name="w_sb")
        w_rows = Wk.rearrange("(a p) k -> p a k", p=P)
        for h in range(2):
            nc.sync.dma_start(out=w_sb[:, 2 * h : 2 * h + 2, :], in_=w_rows[:, 2 * h : 2 * h + 2, :])
        xs = []
        for g in range(NG):
            xg = const.tile([P, 4, D], BF16, name="x%d" % g)
            if g == 0:
                for h in range(2):
                    nc.sync.dma_start(out=xg[:, 2 * h : 2 * h + 2, :], in_=rows[:, 2 * h : 2 * h + 2, :])
            else:
                nc.sync.dma_start(out=xg[:], in_=rows[:, 4 * g : 4 * g + 4, :])
            xs.append(xg)
        one = const.tile([P, 1], F32, name="one")
        nc.vector.memset(one[:], 1.0)
        warm = const.tile([P, 1], F32, name="warm")
        nc.scalar.activation(out=warm[:], in_=one[:], func=ACT.Sqrt)
        ident = const.tile([P, P], F32, name="ident")
        make_identity(nc, ident[:])
        shift = const.tile([P, P], F32, name="shift")
        nc.vector.tensor_copy(out=shift[:, 1:P], in_=ident[:, 0 : P - 1])
        nc.vector.tensor_copy(out=shift[:, 0:1], in_=ident[:, P - 1 : P])
        bias = const.tile([P, D], F32, name="bias")
        part = const.tile([P, 4, NG + 1], F32, name="part")
        w_first = const.tile([P, D], F32, name="w_first")
        w_codes = const.tile([P, D], U32, name="w_codes", align_bytes=64)
        w_scl = const.tile([P, D], U8, name="w_scl", align_bytes=64)
        st = {}

        def ok(g):
            return 0 <= g < NG

        def flip(bank, srcs):
            for h in range(2):
                words = srcs[h].bitcast(F32)
                for u in range(2):
                    nc.tensor.transpose(bank[:, h, u, :], words[:, u * P : (u + 1) * P], ident[:])

        def t1(g, h):
            if ok(g):
                xt = psum.tile([P, 2, 2, P], F32, tag="xt", name="xt")
                flip(xt, [xs[g][:, 2 * h, :], xs[g][:, 2 * h + 1, :]])
                st[("xt", g, h)] = xt

        def cp(g, h):
            if ok(g):
                grp = work.tile([P, 2 * D], BF16, tag="grp", name="grp", align_bytes=64)
                nc.scalar.copy(
                    out=grp[:].bitcast(F32).rearrange("p (a r u) -> p a r u", a=2, r=P, u=2),
                    in_=st[("xt", g, h)][:].rearrange("p h u r -> p h r u"),
                )
                st[("grp", g, h)] = grp

        def qz(g, h):
            if ok(g):
                codes = work.tile([P, 2 * P], U32, tag="codes", name="codes", align_bytes=64)
                scl = work.tile([P, 2 * P], U8, tag="scl", name="scl", align_bytes=64)
                nc.vector.quantize_mx(out=codes[:].bitcast(FP8X4), scales=scl[:], in_=st[("grp", g, h)][:])
                st[("codes", g, h)] = codes
                st[("scl", g, h)] = scl

        def mx(g, a):
            if ok(g):
                acc = psum.tile([P, D], F32, tag="acc", name="acc")
                c0 = (a % 2) * P
                nc.tensor.matmul_mx(
                    out=acc[:],
                    lhsT=st[("codes", g, a // 2)][:, c0 : c0 + P].bitcast(FP8X4),
                    lhsT_scale=st[("scl", g, a // 2)][:, c0 : c0 + P],
                    rhs=w_codes[:].bitcast(FP8X4),
                    rhs_scale=w_scl[:],
                    start=True,
                    stop=True,
                )
                st[("acc", g, a)] = acc

        def p1(g, a):
            if ok(g):
                if a == 0:
                    st[("ssum", g)] = small.tile([P, 4], F32, tag="ssum", name="ssum")
                    st[("n2", g)] = small.tile([P, 4], F32, tag="n2", name="n2")
                if a % 2 == 0:
                    st[("o", g, a // 2)] = work.tile([P, 2, D], F32, tag="o", name="o")
                nc.vector.scalar_tensor_tensor(
                    out=st[("o", g, a // 2)][:, a % 2, :],
                    in0=st[("acc", g, a)][:],
                    scalar=1.0,
                    in1=bias[:],
                    op0=ALU.mult,
                    op1=ALU.add,
                    accum_out=st[("ssum", g)][:, a : a + 1],
                )

        def p2(g, a):
            if ok(g):
                junk = work.tile([P, D], F32, tag="junk", name="junk")
                nc.scalar.activation(
                    out=junk[:],
                    in_=st[("o", g, a // 2)][:, a % 2, :],
                    func=ACT.Square,
                    accum_out=st[("n2", g)][:, a : a + 1],
                )

        def tau(g, h):
            if ok(g):
                tt = work.tile([P, 2, D], F32, tag="tau", name="tt", bufs=4)
                nc.vector.tensor_scalar(
                    out=tt[:], in0=st[("o", g, h)][:], scalar1=DELTA, scalar2=-DELTA, op0=ALU.min, op1=ALU.max
                )
                st[("tau", g, h)] = tt

        def m2(g):
            if ok(g):
                mm = small.tile([P, 4], F32, tag="m2", name="mm")
                nc.vector.tensor_scalar(
                    out=mm[:], in0=st[("n2", g)][:], scalar1=EPS * EPS, scalar2=None, op0=ALU.max
                )
                st[("m2", g)] = mm

        def root(g):
            if ok(g):
                nn = small.tile([P, 4], F32, tag="nn", name="nn")
                nc.scalar.activation(out=nn[:], in_=st[("m2", g)][:], func=ACT.Sqrt)
                st[("nn", g)] = nn

        def rec(g):
            if ok(g):
                rc = small.tile([P, 4], F32, tag="rc", name="rc")
                nc.vector.reciprocal(out=rc[:], in_=st[("nn", g)][:])
                r2 = small.tile([P, 4], F32, tag="r2", name="r2")
                nc.vector.scalar_tensor_tensor(
                    out=r2[:], in0=st[("ssum", g)][:], scalar=1.0 / EPS, in1=rc[:], op0=ALU.mult, op1=ALU.mult
                )
                st[("r2", g)] = r2

        def wt(g, a):
            if ok(g):
                if g == 0 and a == 0:
                    ww = w_first
                else:
                    ww = work.tile([P, D], F32, tag="w", name="ww", bufs=12)
                nc.vector.tensor_scalar(
                    out=ww[:],
                    in0=st[("tau", g, a // 2)][:, a % 2, :],
                    scalar1=st[("r2", g)][:, a : a + 1],
                    scalar2=(1.0 if a % 2 == 0 else -1.0),
                    op0=ALU.mult,
                    op1=ALU.mult,
                )
                st[("w", 4 * g + a)] = ww

        def flip_w(dst, node, perm, j, plain, first, last):
            nc.tensor.matmul(
                out=dst,
                lhsT=st[("w", node)][:, j * P : (j + 1) * P],
                rhs=perm[:],
                is_transpose=(not plain),
                start=first,
                stop=last,
            )

        def ed(g, j):
            if 0 <= g <= NG:
                eb = psum.tile([P, 4, P], F32, tag="e%d" % j, name="eb", bufs=1)
                if g == NG:
                    flip_w(eb[:, 0, :], 0, ident, j, False, True, False)
                    flip_w(eb[:, 0, :], NT - 1, shift, j, False, False, True)
                else:
                    qs = [q for q in range(4) if 4 * g + q >= 1]
                    for q in qs:
                        flip_w(eb[:, q, :], 4 * g + q - 1, ident, j, q == 1, q == qs[0], False)
                    for q in qs:
                        flip_w(eb[:, q, :], 4 * g + q, ident, j, False, False, q == 3)
                st[("e", g, j)] = eb

        def ab(g, j):
            if 0 <= g <= NG:
                flat = st[("e", g, j)][:].rearrange("p q r -> p (q r)")
                lo, hi = 0, D
                if g == 0:
                    lo = P
                if g == NG:
                    lo, hi = 1, P
                junk = work.tile([P, D], F32, tag="junk", name="junk")
                nc.scalar.activation(
                    out=junk[:, lo:hi], in_=flat[:, lo:hi], func=ACT.Abs, accum_out=part[:, j, g : g + 1]
                )

        grp_w = const.tile([P, 4 * D], BF16, name="grp_w", align_bytes=64)
        for h in range(2):
            wb = psum.tile([P, 2, 2, P], F32, tag="e%d" % h, name="wb", bufs=1)
            flip(wb, [w_sb[:, 2 * h, :], w_sb[:, 2 * h + 1, :]])
            nc.vector.tensor_copy(
                out=grp_w[:, 2 * h * D : (2 * h + 2) * D].bitcast(F32).rearrange("p (a r u) -> p a r u", a=2, r=P, u=2),
                in_=wb[:].rearrange("p h u r -> p h r u"),
            )
        nc.vector.quantize_mx(out=w_codes[:].bitcast(FP8X4), scales=w_scl[:], in_=grp_w[:])
        nc.vector.tensor_copy(out=bias[:], in_=b_bf[:])

        for i in range(-2, NG + 4):
            ed(i - 2, 0)
            ab(i - 3, 3)
            p1(i, 0)
            m2(i - 1)
            mx(i, 2)
            p2(i, 0)
            root(i - 1)
            qz(i + 1, 0)
            ed(i - 2, 1)
            t1(i + 1, 1)
            ab(i - 2, 0)
            p1(i, 1)
            mx(i, 3)
            p2(i, 1)
            tau(i, 0)
            rec(i - 1)
            cp(i + 1, 1)
            ed(i - 2, 2)
            t1(i + 2, 0)
            ab(i - 2, 1)
            p1(i, 2)
            p2(i, 2)
            wt(i - 1, 0)
            wt(i - 1, 1)
            cp(i + 2, 0)
            ed(i - 2, 3)
            p1(i, 3)
            mx(i + 1, 0)
            mx(i + 1, 1)
            p2(i, 3)
            ab(i - 2, 2)
            wt(i - 1, 2)
            wt(i - 1, 3)
            tau(i, 1)
            qz(i + 1, 1)

        dcol = small.tile([P, 4], F32, tag="dcol", name="dcol")
        nc.vector.tensor_reduce(out=dcol[:], in_=part[:], axis=AX.X, op=ALU.add)
        fin = psum.tile([P, D], F32, tag="acc", name="fin")
        for j in range(4):
            nc.tensor.transpose(fin[:, j * P : (j + 1) * P], dcol[:, j : j + 1].to_broadcast([P, P]), ident[:])
        res = const.tile([P, D], F32, name="res")
        nc.vector.tensor_copy(out=res[:], in_=fin[:])
        for a in range(4):
            eng = nc.sync if a % 2 == 0 else nc.scalar
            eng.dma_start(out=out[a * P : (a + 1) * P, :], in_=res[:])
